import numpy as np
import ml_dtypes


def mxq(x, axis, fmt="e4m3"):
    dtype, down = {"e4m3": (ml_dtypes.float8_e4m3fn, 7), "e5m2": (ml_dtypes.float8_e5m2, 14)}[fmt]
    v = np.moveaxis(np.asarray(x, np.float32).astype(ml_dtypes.bfloat16).astype(np.float64), axis, -1)
    blocks = v.reshape(v.shape[:-1] + (-1, 32))
    amax = np.abs(blocks).max(-1, keepdims=True)
    byte = np.maximum(np.where(amax > 0, np.frexp(amax)[1] - 1 + 127, 0) - down, 1)
    scale = np.exp2(byte - 127.0)
    codes = (blocks / scale).astype(np.float32).astype(dtype).astype(np.float64)
    return np.moveaxis((codes * scale).reshape(v.shape), -1, axis)


WIDE = False


def mx_kscale(k):
    if not WIDE:
        return np.ones(k)
    levels = np.array([10, -10, 5, -5, 0])
    a = np.random.permutation(np.resize(levels, k // 512 * 4)).reshape(k // 512, 4)
    idx = np.arange(k)
    return np.exp2(a[idx // 512, idx % 128 // 32])


BF16 = ml_dtypes.bfloat16


def bf(x):
    return np.asarray(x, np.float32).astype(BF16)


def f64(x):
    return np.asarray(x).astype(np.float64)


B, S, IN, OUT, R, RT = 2, 256, 2048, 2048, 512, 64


def setup_inputs():
    r, t = mx_kscale(R), mx_kscale(IN)
    return {
        "x": bf(np.random.standard_normal((B, S, IN)) * t),
        "siva_u_t": bf(np.random.standard_normal((OUT, RT)) * 1.7 / np.sqrt(R) * r[:RT]),
        "siva_u_d": bf(np.random.standard_normal((OUT, R - RT)) * 1.7 / np.sqrt(R) * r[RT:]),
        "siva_s": bf(np.random.uniform(0.0, 1.0, R)),
        "siva_v_t": bf(np.random.standard_normal((RT, IN)) / np.sqrt(IN) / r[:RT, None] / t),
        "siva_v_d": bf(np.random.standard_normal((R - RT, IN)) / np.sqrt(IN) / r[RT:, None] / t),
        "bias": bf(np.random.standard_normal(OUT) * 0.5),
    }


def reference(x, siva_u_t, siva_u_d, siva_s, siva_v_t, siva_v_d, bias):
    siva_u = np.concatenate((f64(siva_u_t), f64(siva_u_d)), axis=1)
    siva_v = np.concatenate((f64(siva_v_t), f64(siva_v_d)), axis=0)
    weight = mxq(siva_u * f64(siva_s), 1, "e4m3") @ mxq(siva_v, 0, "e4m3")
    return (mxq(f64(x), 2, "e4m3") @ mxq(weight, 1, "e4m3").T) + f64(bias)

@@ -1,0 +1,256 @@
+from contextlib import ExitStack
+
+import concourse.bass as bass
+import concourse.mybir as mybir
+import concourse.tile as tile
+from concourse.masks import make_identity
+
+F32 = mybir.dt.float32
+BF16 = mybir.dt.bfloat16
+U32 = mybir.dt.uint32
+U8 = mybir.dt.uint8
+FP8X4 = mybir.dt.float8_e4m3fn_x4
+ALU = mybir.AluOpType
+
+P = 128
+TOK = 512
+IN = 2048
+OUT = 2048
+R = 512
+RT = 64
+NG = 4
+NC = 4
+NM = 4
+LAG = 2
+
+FLOPS = 2 * OUT * IN * R + 2 * TOK * IN * OUT
+
+
+def tile_sivalinear_kernel(tc, x, siva_u_t, siva_u_d, siva_s, siva_v_t, siva_v_d, bias, out):
+    nc = tc.nc
+    xf = x.flatten_outer_dims()
+    of = out.flatten_outer_dims()
+
+    with ExitStack() as ctx:
+        const = ctx.enter_context(tc.tile_pool(name="const", bufs=1))
+        raw = ctx.enter_context(tc.tile_pool(name="raw", bufs=1))
+        grp = ctx.enter_context(tc.tile_pool(name="grp", bufs=2))
+        wgp = ctx.enter_context(tc.tile_pool(name="wgp", bufs=4))
+        keep = ctx.enter_context(tc.tile_pool(name="keep", bufs=1))
+        resp = ctx.enter_context(tc.tile_pool(name="resp", bufs=4))
+        psum = ctx.enter_context(tc.psum_pool(name="psum", bufs=4))
+
+        s4 = const.tile([P, 4], BF16, name="s4")
+        nc.scalar.dma_start(
+            out=s4[:].rearrange("p (h e) -> p h e", h=2),
+            in_=siva_s.rearrange("(h p e) -> p h e", h=2, e=2),
+        )
+        ident = const.tile([P, P], F32, name="ident")
+        make_identity(nc, ident[:])
+
+        v_raw = [raw.tile([P, 4 * 512], BF16, name="v_raw%d" % g) for g in range(NG)]
+        u_raw = [raw.tile([P, 4 * R], BF16, name="u_raw%d" % c) for c in range(NC)]
+        x_raw = [raw.tile([P, NM * 512], BF16, name="x_raw%d" % g) for g in range(NG)]
+
+        def load_v(g):
+            cols = slice(512 * g, 512 * g + 512)
+            lo = v_raw[g][:, 0:1024].rearrange("q (e i) -> q e i", e=2)
+            hi = v_raw[g][:, 1024:2048].rearrange("q (e i) -> q e i", e=2)
+            nc.sync.dma_start(out=lo[0:32], in_=siva_v_t[:, cols].rearrange("(q e) i -> q e i", e=2))
+            nc.sync.dma_start(out=lo[32:128], in_=siva_v_d[0:192, cols].rearrange("(q e) i -> q e i", e=2))
+            nc.sync.dma_start(out=hi, in_=siva_v_d[192:448, cols].rearrange("(q e) i -> q e i", e=2))
+
+        def load_u(c):
+            rows = slice(512 * c, 512 * c + 512)
+            dst = u_raw[c][:].rearrange("p (a r) -> p a r", a=4)
+            nc.sync.dma_start(out=dst[:, :, 0:RT], in_=siva_u_t[rows, :].rearrange("(a p) r -> p a r", p=P))
+            nc.sync.dma_start(out=dst[:, :, RT:R], in_=siva_u_d[rows, :].rearrange("(a p) r -> p a r", p=P))
+
+        def load_x(g):
+            cols = slice(512 * g, 512 * g + 512)
+            nc.sync.dma_start(
+                out=x_raw[g][:].rearrange("p (m i) -> p m i", m=NM),
+                in_=xf[:, cols].rearrange("(m p) i -> p m i", p=P),
+            )
+
+        load_v(0)
+        load_u(0)
+        load_x(0)
+        for g in range(1, NG):
+            load_v(g)
+            load_x(g)
+        for c in range(1, NC):
+            load_u(c)
+        bias_bc = const.tile([P, OUT], BF16, name="bias_bc")
+        nc.sync.dma_start(out=bias_bc[:], in_=bias.partition_broadcast(P))
+
+        def codes(name):
+            return (
+                keep.tile([P, 512], U32, name=name + "_c", align_bytes=64),
+                keep.tile([P, 512], U8, name=name + "_s", align_bytes=64),
+            )
+
+        u_q = [codes("u%d" % c) for c in range(NC)]
+        v_q = [codes("v%d" % g) for g in range(NG)]
+        x_q = [codes("x%d" % g) for g in range(NG)]
+        w_q = [codes("w%d" % s) for s in range(NC * NG)]
+
+        def quantise(dst, src):
+            nc.vector.quantize_mx(out=dst[0][:].bitcast(FP8X4), scales=dst[1][:], in_=src[:])
+
+        s4_b = s4[:].rearrange("p (o h e) -> p o h e", o=1, h=2).to_broadcast([P, P, 2, 2])
+
+        state = {}
+
+        def t_u(c):
+            words = u_raw[c][:].bitcast(F32)
+            banks = []
+            for b in range(2):
+                pt = psum.tile([P, 512], F32, name="pt_u", tag="w")
+                for sl in range(2):
+                    a = 2 * b + sl
+                    for h in range(2):
+                        nc.tensor.transpose(
+                            pt[:, 256 * sl + 128 * h : 256 * sl + 128 * h + 128],
+                            words[:, 256 * a + 128 * h : 256 * a + 128 * h + 128],
+                            ident[:],
+                        )
+                banks.append(pt)
+            state["tu%d" % c] = banks
+
+        def e_u(c):
+            ug = grp.tile([P, 2048], BF16, name="ug", tag="ug", align_bytes=64)
+            for b in range(2):
+                pt = state["tu%d" % c][b]
+                view = pt[:].bitcast(BF16).rearrange("p (s h o e) -> p s o h e", s=2, h=2, e=2)
+                for sl in range(2):
+                    a = 2 * b + sl
+                    nc.vector.tensor_tensor(
+                        out=ug[:, 512 * a : 512 * a + 512].rearrange("p (o h e) -> p o h e", h=2, e=2),
+                        in0=view[:, sl],
+                        in1=s4_b,
+                        op=ALU.mult,
+                    )
+            state["ug%d" % c] = ug
+
+        def q_u(c):
+            quantise(u_q[c], state["ug%d" % c])
+
+        def r_v(g):
+            vg = grp.tile([P, 2048], BF16, name="vg", tag="vg", align_bytes=64)
+            src = v_raw[g][:].rearrange("p (j h q e) -> p e h q j", j=4, h=2, e=2)
+            dst = vg[:].rearrange("p (h e q j) -> p e h q j", h=2, e=2, j=4)
+            for e in range(2):
+                nc.vector.tensor_copy(out=dst[:, e], in_=src[:, e])
+            state["vg%d" % g] = vg
+
+        def q_v(g):
+            quantise(v_q[g], state["vg%d" % g])
+
+        def t_x(g):
+            words = x_raw[g][:].bitcast(F32)
+            banks = []
+            for b in range(2):
+                pt = psum.tile([P, 512], F32, name="pt_x", tag="w")
+                for sl in range(2):
+                    m = 2 * b + sl
+                    for h in range(2):
+                        nc.tensor.transpose(
+                            pt[:, 256 * sl + 128 * h : 256 * sl + 128 * h + 128],
+                            words[:, 256 * m + 128 * h : 256 * m + 128 * h + 128],
+                            ident[:],
+                        )
+                banks.append(pt)
+            state["tx%d" % g] = banks
+
+        def e_x(g):
+            xg = grp.tile([P, 2048], BF16, name="xg", tag="xg", align_bytes=64)
+            xw = xg[:].bitcast(F32)
+            for b in range(2):
+                pt = state["tx%d" % g][b]
+                nc.scalar.copy(
+                    out=xw[:, 512 * b : 512 * b + 512].rearrange("p (s k h) -> p s k h", s=2, h=2),
+                    in_=pt[:].rearrange("p (s h k) -> p s k h", s=2, h=2),
+                )
+            state["xg%d" % g] = xg
+
+        def q_x(g):
+            quantise(x_q[g], state["xg%d" % g])
+
+        def m1(s):
+            c, g = divmod(s, NG)
+            wg = wgp.tile([P, 2048], BF16, name="wg", tag="wg", align_bytes=64)
+            for a in range(4):
+                pw = psum.tile([P, 512], F32, name="pw", tag="w")
+                for t in range(4):
+                    nc.tensor.matmul_mx(
+                        out=pw[:, 128 * t : 128 * t + 128],
+                        lhsT=v_q[g][0][:, 128 * t : 128 * t + 128].bitcast(FP8X4),
+                        lhsT_scale=v_q[g][1][:, 128 * t : 128 * t + 128],
+                        rhs=u_q[c][0][:, 128 * a : 128 * a + 128].bitcast(FP8X4),
+                        rhs_scale=u_q[c][1][:, 128 * a : 128 * a + 128],
+                        start=True,
+                        stop=True,
+                    )
+                nc.scalar.copy(
+                    out=wg[:, 512 * a : 512 * a + 512].rearrange("p (o t) -> p o t", t=4),
+                    in_=pw[:].rearrange("p (t o) -> p o t", t=4),
+                )
+            state["wg%d" % s] = wg
+
+        def q_w(s):
+            quantise(w_q[s], state["wg%d" % s])
+
+        def m2(s):
+            c, g = divmod(s, NG)
+            if g == 0:
+                state["po"] = [psum.tile([P, 512], F32, name="po", tag="o") for m in range(NM)]
+            for m in range(NM):
+                nc.tensor.matmul_mx(
+                    out=state["po"][m][:],
+                    lhsT=x_q[g][0][:, 128 * m : 128 * m + 128].bitcast(FP8X4),
+                    lhsT_scale=x_q[g][1][:, 128 * m : 128 * m + 128],
+                    rhs=w_q[s][0][:].bitcast(FP8X4),
+                    rhs_scale=w_q[s][1][:],
+                    start=(g == 0),
+                    stop=(g == NG - 1),
+                )
+            if g == NG - 1:
+                for m in range(NM):
+                    res = resp.tile([P, 512], F32, name="res", tag="res")
+                    nc.vector.tensor_tensor(
+                        out=res[:],
+                        in0=state["po"][m][:],
+                        in1=bias_bc[:, 512 * c : 512 * c + 512],
+                        op=ALU.add,
+                    )
+                    nc.sync.dma_start(out=of[128 * m : 128 * m + 128, 512 * c : 512 * c + 512], in_=res[:])
+
+        r_v(0)
+        t_u(0)
+        e_u(0)
+        q_v(0)
+        q_u(0)
+        t_x(0)
+        e_x(0)
+        steps = NC * NG
+        for s in range(steps + LAG):
+            if s < steps:
+                m1(s)
+            if s < 3:
+                r_v(s + 1)
+                q_x(s)
+                q_v(s + 1)
+                t_x(s + 1)
+                e_x(s + 1)
+            if s == 3:
+                q_x(3)
+            if s % 4 == 1 and s // 4 + 1 < NC:
+                t_u(s // 4 + 1)
+                e_u(s // 4 + 1)
+            if s % 4 == 2 and s // 4 + 1 < NC:
+                q_u(s // 4 + 1)
+            if 1 <= s <= steps:
+                q_w(s - 1)
+            if s >= LAG:
+                m2(s - LAG)

@@ -1,8 +1,6 @@
 from contextlib import ExitStack
 
-import concourse.bass as bass
 import concourse.mybir as mybir
-import concourse.tile as tile
 from concourse.masks import make_identity
 
 F32 = mybir.dt.float32
@@ -21,7 +19,10 @@ RT = 64
 NG = 4
 NC = 4
 NM = 4
-LAG = 2
+STEPS = NC * NG
+LAGS = (1, 2, 2, 3)
+M_ORDER = (3, 2, 1, 0)
+V_EVERY = 2
 
 FLOPS = 2 * OUT * IN * R + 2 * TOK * IN * OUT
 
@@ -39,6 +40,8 @@ def tile_sivalinear_kernel(tc, x, siva_u_t, siva_u_d, siva_s, siva_v_t, siva_v_d
         keep = ctx.enter_context(tc.tile_pool(name="keep", bufs=1))
         resp = ctx.enter_context(tc.tile_pool(name="resp", bufs=4))
         psum = ctx.enter_context(tc.psum_pool(name="psum", bufs=4))
+        psum_o = ctx.enter_context(tc.psum_pool(name="psum_o", bufs=1))
+        ctx.enter_context(tc.manual_schedule())
 
         s4 = const.tile([P, 4], BF16, name="s4")
         nc.scalar.dma_start(
@@ -60,9 +63,9 @@ def tile_sivalinear_kernel(tc, x, siva_u_t, siva_u_d, siva_s, siva_v_t, siva_v_d
             nc.sync.dma_start(out=lo[32:128], in_=siva_v_d[0:192, cols].rearrange("(q e) i -> q e i", e=2))
             nc.sync.dma_start(out=hi, in_=siva_v_d[192:448, cols].rearrange("(q e) i -> q e i", e=2))
 
-        def load_u(c):
-            rows = slice(512 * c, 512 * c + 512)
-            dst = u_raw[c][:].rearrange("p (a r) -> p a r", a=4)
+        def load_u(c, a0, a1):
+            rows = slice(512 * c + 128 * a0, 512 * c + 128 * a1)
+            dst = u_raw[c][:].rearrange("p (a r) -> p a r", a=4)[:, a0:a1]
             nc.sync.dma_start(out=dst[:, :, 0:RT], in_=siva_u_t[rows, :].rearrange("(a p) r -> p a r", p=P))
             nc.sync.dma_start(out=dst[:, :, RT:R], in_=siva_u_d[rows, :].rearrange("(a p) r -> p a r", p=P))
 
@@ -74,15 +77,20 @@ def tile_sivalinear_kernel(tc, x, siva_u_t, siva_u_d, siva_s, siva_v_t, siva_v_d
             )
 
         load_v(0)
-        load_u(0)
+        load_u(0, 0, 2)
+        load_u(0, 2, 4)
+        load_v(1)
         load_x(0)
-        for g in range(1, NG):
-            load_v(g)
-            load_x(g)
-        for c in range(1, NC):
-            load_u(c)
+        load_v(2)
+        load_x(1)
+        load_v(3)
+        load_x(2)
+        load_u(1, 0, 4)
+        load_x(3)
         bias_bc = const.tile([P, OUT], BF16, name="bias_bc")
         nc.sync.dma_start(out=bias_bc[:], in_=bias.partition_broadcast(P))
+        load_u(2, 0, 4)
+        load_u(3, 0, 4)
 
         def codes(name):
             return (
@@ -93,164 +101,172 @@ def tile_sivalinear_kernel(tc, x, siva_u_t, siva_u_d, siva_s, siva_v_t, siva_v_d
         u_q = [codes("u%d" % c) for c in range(NC)]
         v_q = [codes("v%d" % g) for g in range(NG)]
         x_q = [codes("x%d" % g) for g in range(NG)]
-        w_q = [codes("w%d" % s) for s in range(NC * NG)]
+        w_q = [codes("w%d" % s) for s in range(STEPS)]
 
-        def quantise(dst, src):
-            nc.vector.quantize_mx(out=dst[0][:].bitcast(FP8X4), scales=dst[1][:], in_=src[:])
+        def quantise(dst, src, lo=0, hi=512):
+            nc.vector.quantize_mx(
+                out=dst[0][:, lo:hi].bitcast(FP8X4), scales=dst[1][:, lo:hi], in_=src[:, 4 * lo : 4 * hi]
+            )
 
         s4_b = s4[:].rearrange("p (o h e) -> p o h e", o=1, h=2).to_broadcast([P, P, 2, 2])
 
         state = {}
 
-        def t_u(c):
-            words = u_raw[c][:].bitcast(F32)
-            banks = []
-            for b in range(2):
-                pt = psum.tile([P, 512], F32, name="pt_u", tag="w")
-                for sl in range(2):
-                    a = 2 * b + sl
-                    for h in range(2):
-                        nc.tensor.transpose(
-                            pt[:, 256 * sl + 128 * h : 256 * sl + 128 * h + 128],
-                            words[:, 256 * a + 128 * h : 256 * a + 128 * h + 128],
-                            ident[:],
-                        )
-                banks.append(pt)
-            state["tu%d" % c] = banks
+        def transposes(src, b):
+            words = src[:].bitcast(F32)
+            pt = psum.tile([P, 512], F32, name="pt", tag="w")
+            for sl in range(2):
+                for h in range(2):
+                    lo = 256 * sl + 128 * h
+                    nc.tensor.transpose(pt[:, lo : lo + 128], words[:, 512 * b + lo : 512 * b + lo + 128], ident[:])
+            return pt
 
-        def e_u(c):
-            ug = grp.tile([P, 2048], BF16, name="ug", tag="ug", align_bytes=64)
-            for b in range(2):
-                pt = state["tu%d" % c][b]
-                view = pt[:].bitcast(BF16).rearrange("p (s h o e) -> p s o h e", s=2, h=2, e=2)
-                for sl in range(2):
-                    a = 2 * b + sl
-                    nc.vector.tensor_tensor(
-                        out=ug[:, 512 * a : 512 * a + 512].rearrange("p (o h e) -> p o h e", h=2, e=2),
-                        in0=view[:, sl],
-                        in1=s4_b,
-                        op=ALU.mult,
-                    )
-            state["ug%d" % c] = ug
+        def t_u(c, b):
+            state["tu", c, b] = transposes(u_raw[c], b)
 
-        def q_u(c):
-            quantise(u_q[c], state["ug%d" % c])
+        def e_u(c, b):
+            if b == 0:
+                state["ug", c] = grp.tile([P, 2048], BF16, name="ug", tag="ug", align_bytes=64)
+            ug = state["ug", c]
+            view = state["tu", c, b][:].bitcast(BF16).rearrange("p (s h o e) -> p s o h e", s=2, h=2, e=2)
+            for sl in range(2):
+                a = 2 * b + sl
+                nc.vector.tensor_tensor(
+                    out=ug[:, 512 * a : 512 * a + 512].rearrange("p (o h e) -> p o h e", h=2, e=2),
+                    in0=view[:, sl],
+                    in1=s4_b,
+                    op=ALU.mult,
+                )
 
-        def r_v(g):
-            vg = grp.tile([P, 2048], BF16, name="vg", tag="vg", align_bytes=64)
-            src = v_raw[g][:].rearrange("p (j h q e) -> p e h q j", j=4, h=2, e=2)
-            dst = vg[:].rearrange("p (h e q j) -> p e h q j", h=2, e=2, j=4)
-            for e in range(2):
-                nc.vector.tensor_copy(out=dst[:, e], in_=src[:, e])
-            state["vg%d" % g] = vg
+        def q_u(c, lo=0, hi=512):
+            quantise(u_q[c], state["ug", c], lo, hi)
+
+        def r_v(g, h, eng):
+            if h == 0:
+                state["vg", g] = grp.tile([P, 2048], BF16, name="vg", tag="vg", align_bytes=64)
+            src = v_raw[g][:].rearrange("p (j h q e) -> p h e q j", j=4, h=2, e=2)
+            dst = state["vg", g][:].rearrange("p (h e q j) -> p h e q j", h=2, e=2, j=4)
+            if eng == "v":
+                nc.vector.tensor_copy(out=dst[:, h], in_=src[:, h])
+            else:
+                nc.scalar.copy(out=dst[:, h], in_=src[:, h])
 
         def q_v(g):
-            quantise(v_q[g], state["vg%d" % g])
+            quantise(v_q[g], state["vg", g])
 
-        def t_x(g):
-            words = x_raw[g][:].bitcast(F32)
-            banks = []
-            for b in range(2):
-                pt = psum.tile([P, 512], F32, name="pt_x", tag="w")
-                for sl in range(2):
-                    m = 2 * b + sl
-                    for h in range(2):
-                        nc.tensor.transpose(
-                            pt[:, 256 * sl + 128 * h : 256 * sl + 128 * h + 128],
-                            words[:, 256 * m + 128 * h : 256 * m + 128 * h + 128],
-                            ident[:],
-                        )
-                banks.append(pt)
-            state["tx%d" % g] = banks
+        def t_x(g, b):
+            state["tx", g, b] = transposes(x_raw[g], b)
 
-        def e_x(g):
-            xg = grp.tile([P, 2048], BF16, name="xg", tag="xg", align_bytes=64)
-            xw = xg[:].bitcast(F32)
-            for b in range(2):
-                pt = state["tx%d" % g][b]
-                nc.scalar.copy(
-                    out=xw[:, 512 * b : 512 * b + 512].rearrange("p (s k h) -> p s k h", s=2, h=2),
-                    in_=pt[:].rearrange("p (s h k) -> p s k h", s=2, h=2),
-                )
-            state["xg%d" % g] = xg
+        def e_x(g, b, eng):
+            if b == 0:
+                state["xg", g] = grp.tile([P, 2048], BF16, name="xg", tag="xg", align_bytes=64)
+            xw = state["xg", g][:].bitcast(F32)
+            dst = xw[:, 512 * b : 512 * b + 512].rearrange("p (s k h) -> p s k h", s=2, h=2)
+            src = state["tx", g, b][:].rearrange("p (s h k) -> p s k h", s=2, h=2)
+            if eng == "v":
+                nc.vector.tensor_copy(out=dst, in_=src)
+            else:
+                nc.scalar.copy(out=dst, in_=src)
 
         def q_x(g):
-            quantise(x_q[g], state["xg%d" % g])
+            quantise(x_q[g], state["xg", g])
 
-        def m1(s):
+        def m1(s, a):
             c, g = divmod(s, NG)
-            wg = wgp.tile([P, 2048], BF16, name="wg", tag="wg", align_bytes=64)
-            for a in range(4):
-                pw = psum.tile([P, 512], F32, name="pw", tag="w")
-                for t in range(4):
-                    nc.tensor.matmul_mx(
-                        out=pw[:, 128 * t : 128 * t + 128],
-                        lhsT=v_q[g][0][:, 128 * t : 128 * t + 128].bitcast(FP8X4),
-                        lhsT_scale=v_q[g][1][:, 128 * t : 128 * t + 128],
-                        rhs=u_q[c][0][:, 128 * a : 128 * a + 128].bitcast(FP8X4),
-                        rhs_scale=u_q[c][1][:, 128 * a : 128 * a + 128],
-                        start=True,
-                        stop=True,
-                    )
-                nc.scalar.copy(
-                    out=wg[:, 512 * a : 512 * a + 512].rearrange("p (o t) -> p o t", t=4),
-                    in_=pw[:].rearrange("p (t o) -> p o t", t=4),
+            pw = psum.tile([P, 512], F32, name="pw", tag="w")
+            for t in range(4):
+                nc.tensor.matmul_mx(
+                    out=pw[:, 128 * t : 128 * t + 128],
+                    lhsT=v_q[g][0][:, 128 * t : 128 * t + 128].bitcast(FP8X4),
+                    lhsT_scale=v_q[g][1][:, 128 * t : 128 * t + 128],
+                    rhs=u_q[c][0][:, 128 * a : 128 * a + 128].bitcast(FP8X4),
+                    rhs_scale=u_q[c][1][:, 128 * a : 128 * a + 128],
+                    start=True,
+                    stop=True,
                 )
-            state["wg%d" % s] = wg
+            state["pw", s, a] = pw
 
-        def q_w(s):
-            quantise(w_q[s], state["wg%d" % s])
+        def e_w(s, a, eng):
+            if a == 0:
+                state["wg", s] = wgp.tile([P, 2048], BF16, name="wg", tag="wg", align_bytes=64)
+            dst = state["wg", s][:, 512 * a : 512 * a + 512].rearrange("p (o t) -> p o t", t=4)
+            src = state["pw", s, a][:].rearrange("p (t o) -> p o t", t=4)
+            if eng == "v":
+                nc.vector.tensor_copy(out=dst, in_=src)
+            else:
+                nc.scalar.copy(out=dst, in_=src)
 
-        def m2(s):
+        def q_w(s, lo=0, hi=512):
+            quantise(w_q[s], state["wg", s], lo, hi)
+
+        def m2(s, m):
             c, g = divmod(s, NG)
             if g == 0:
-                state["po"] = [psum.tile([P, 512], F32, name="po", tag="o") for m in range(NM)]
-            for m in range(NM):
-                nc.tensor.matmul_mx(
-                    out=state["po"][m][:],
-                    lhsT=x_q[g][0][:, 128 * m : 128 * m + 128].bitcast(FP8X4),
-                    lhsT_scale=x_q[g][1][:, 128 * m : 128 * m + 128],
-                    rhs=w_q[s][0][:].bitcast(FP8X4),
-                    rhs_scale=w_q[s][1][:],
-                    start=(g == 0),
-                    stop=(g == NG - 1),
-                )
-            if g == NG - 1:
-                for m in range(NM):
-                    res = resp.tile([P, 512], F32, name="res", tag="res")
-                    nc.vector.tensor_tensor(
-                        out=res[:],
-                        in0=state["po"][m][:],
-                        in1=bias_bc[:, 512 * c : 512 * c + 512],
-                        op=ALU.add,
-                    )
-                    nc.sync.dma_start(out=of[128 * m : 128 * m + 128, 512 * c : 512 * c + 512], in_=res[:])
+                state["po", m] = psum_o.tile([P, 512], F32, name="po%d" % m, tag="o%d" % m)
+            nc.tensor.matmul_mx(
+                out=state["po", m][:],
+                lhsT=x_q[g][0][:, 128 * m : 128 * m + 128].bitcast(FP8X4),
+                lhsT_scale=x_q[g][1][:, 128 * m : 128 * m + 128],
+                rhs=w_q[s][0][:].bitcast(FP8X4),
+                rhs_scale=w_q[s][1][:],
+                start=(g == 0),
+                stop=(g == NG - 1),
+            )
 
-        r_v(0)
-        t_u(0)
-        e_u(0)
+        def e_o(c, m):
+            res = resp.tile([P, 512], F32, name="res", tag="res")
+            nc.vector.tensor_tensor(
+                out=res[:], in0=state["po", m][:], in1=bias_bc[:, 512 * c : 512 * c + 512], op=ALU.add
+            )
+            nc.sync.dma_start(out=of[128 * m : 128 * m + 128, 512 * c : 512 * c + 512], in_=res[:])
+
+        r_v(0, 0, "v")
+        r_v(0, 1, "s")
+        t_u(0, 0)
         q_v(0)
-        q_u(0)
-        t_x(0)
-        e_x(0)
-        steps = NC * NG
-        for s in range(steps + LAG):
-            if s < steps:
-                m1(s)
-            if s < 3:
-                r_v(s + 1)
-                q_x(s)
+        e_u(0, 0)
+        t_u(0, 1)
+        q_u(0, 0, 256)
+        e_u(0, 1)
+        q_u(0, 256, 512)
+        for s in range(STEPS):
+            c, g = divmod(s, NG)
+            last = s == STEPS - 1
+            if s + 1 < NG:
+                r_v(s + 1, 0, "v")
+                r_v(s + 1, 1, "v")
                 q_v(s + 1)
-                t_x(s + 1)
-                e_x(s + 1)
-            if s == 3:
-                q_x(3)
-            if s % 4 == 1 and s // 4 + 1 < NC:
-                t_u(s // 4 + 1)
-                e_u(s // 4 + 1)
-            if s % 4 == 2 and s // 4 + 1 < NC:
-                q_u(s // 4 + 1)
-            if 1 <= s <= steps:
+            if 1 <= s:
                 q_w(s - 1)
-            if s >= LAG:
-                m2(s - LAG)
+            if 1 <= s <= NG:
+                q_x(s - 1)
+            if g == 3 and c + 1 < NC:
+                q_u(c + 1)
+            for a in range(4):
+                m1(s, a)
+                e_w(s, a, "v" if ((a == 3 and s >= NG and s % V_EVERY == 1) or (last and a == 1)) else "s")
+                if last and a % 2 == 1:
+                    q_w(s, 128 * (a - 1), 128 * (a + 1))
+            if s < NG:
+                for b in range(2):
+                    t_x(s, b)
+                    e_x(s, b, "s")
+            if g == 2 and c + 1 < NC:
+                for b in range(2):
+                    t_u(c + 1, b)
+                    e_u(c + 1, b)
+            closed = []
+            for m in M_ORDER:
+                sm = s - LAGS[m]
+                if 0 <= sm:
+                    m2(sm, m)
+                    if sm % NG == NG - 1:
+                        closed.append((sm // NG, m))
+            for cm in closed:
+                e_o(cm[0], cm[1])
+        for m in M_ORDER:
+            for sm in range(STEPS - LAGS[m], STEPS - 1):
+                m2(sm, m)
+        for m in M_ORDER:
+            m2(STEPS - 1, m)
+            e_o(NC - 1, m)

@@ -7,6 +7,7 @@ F32 = mybir.dt.float32
 BF16 = mybir.dt.bfloat16
 U32 = mybir.dt.uint32
 U8 = mybir.dt.uint8
+I32 = mybir.dt.int32
 FP8X4 = mybir.dt.float8_e4m3fn_x4
 ALU = mybir.AluOpType
 
@@ -43,6 +44,12 @@ def tile_sivalinear_kernel(tc, x, siva_u_t, siva_u_d, siva_s, siva_v_t, siva_v_d
         psum_o = ctx.enter_context(tc.psum_pool(name="psum_o", bufs=1))
         ctx.enter_context(tc.manual_schedule())
 
+        bias_row = const.tile([P, OUT], BF16, name="bias_row")
+        nc.vector.memset(bias_row[:].bitcast(I32), 0)
+        nc.scalar.dma_start(out=bias_row[0:1, :], in_=bias.rearrange("(o n) -> o n", o=1))
+        ones = const.tile([P, P], BF16, name="ones")
+        nc.vector.memset(ones[:], 1.0)
+        bias_bc = const.tile([P, OUT], F32, name="bias_bc")
         s4 = const.tile([P, 4], BF16, name="s4")
         nc.scalar.dma_start(
             out=s4[:].rearrange("p (h e) -> p h e", h=2),
@@ -87,8 +94,6 @@ def tile_sivalinear_kernel(tc, x, siva_u_t, siva_u_d, siva_s, siva_v_t, siva_v_d
         load_x(2)
         load_u(1, 0, 4)
         load_x(3)
-        bias_bc = const.tile([P, OUT], BF16, name="bias_bc")
-        nc.sync.dma_start(out=bias_bc[:], in_=bias.partition_broadcast(P))
         load_u(2, 0, 4)
         load_u(3, 0, 4)
 
@@ -220,8 +225,20 @@ def tile_sivalinear_kernel(tc, x, siva_u_t, siva_u_d, siva_s, siva_v_t, siva_v_d
             )
             nc.sync.dma_start(out=of[128 * m : 128 * m + 128, 512 * c : 512 * c + 512], in_=res[:])
 
+        def b_mm(c):
+            pb = psum_o.tile([P, 512], F32, name="pb%d" % c, tag="o%d" % c)
+            nc.tensor.matmul(out=pb[:], lhsT=ones[:], rhs=bias_row[:, 512 * c : 512 * c + 512], start=True, stop=True)
+            state["pb", c] = pb
+
+        def b_ev(c):
+            nc.scalar.copy(out=bias_bc[:, 512 * c : 512 * c + 512], in_=state["pb", c][:])
+
+        for c in range(NC):
+            b_mm(c)
         r_v(0, 0, "v")
         r_v(0, 1, "s")
+        for c in range(NC):
+            b_ev(c)
         t_u(0, 0)
         q_v(0)
         e_u(0, 0)

@@ -7,7 +7,6 @@ F32 = mybir.dt.float32
 BF16 = mybir.dt.bfloat16
 U32 = mybir.dt.uint32
 U8 = mybir.dt.uint8
-I32 = mybir.dt.int32
 FP8X4 = mybir.dt.float8_e4m3fn_x4
 ALU = mybir.AluOpType
 
@@ -44,17 +43,15 @@ def tile_sivalinear_kernel(tc, x, siva_u_t, siva_u_d, siva_s, siva_v_t, siva_v_d
         psum_o = ctx.enter_context(tc.psum_pool(name="psum_o", bufs=1))
         ctx.enter_context(tc.manual_schedule())
 
-        bias_row = const.tile([P, OUT], BF16, name="bias_row")
-        nc.vector.memset(bias_row[:].bitcast(I32), 0)
-        nc.scalar.dma_start(out=bias_row[0:1, :], in_=bias.rearrange("(o n) -> o n", o=1))
-        ones = const.tile([P, P], BF16, name="ones")
-        nc.vector.memset(ones[:], 1.0)
-        bias_bc = const.tile([P, OUT], F32, name="bias_bc")
         s4 = const.tile([P, 4], BF16, name="s4")
         nc.scalar.dma_start(
             out=s4[:].rearrange("p (h e) -> p h e", h=2),
             in_=siva_s.rearrange("(h p e) -> p h e", h=2, e=2),
         )
+        warm_in = const.tile([P, 1], F32, name="warm_in")
+        warm_out = const.tile([P, 1], F32, name="warm_out")
+        nc.vector.memset(warm_in[:], 0.0)
+        nc.scalar.copy(out=warm_out[:], in_=warm_in[:])
         ident = const.tile([P, P], F32, name="ident")
         make_identity(nc, ident[:])
 
@@ -83,8 +80,9 @@ def tile_sivalinear_kernel(tc, x, siva_u_t, siva_u_d, siva_s, siva_v_t, siva_v_d
                 in_=xf[:, cols].rearrange("(m p) i -> p m i", p=P),
             )
 
+        load_u(0, 0, 1)
         load_v(0)
-        load_u(0, 0, 2)
+        load_u(0, 1, 2)
         load_u(0, 2, 4)
         load_v(1)
         load_x(0)
@@ -94,6 +92,8 @@ def tile_sivalinear_kernel(tc, x, siva_u_t, siva_u_d, siva_s, siva_v_t, siva_v_d
         load_x(2)
         load_u(1, 0, 4)
         load_x(3)
+        bias_bc = const.tile([P, OUT], BF16, name="bias_bc")
+        nc.sync.dma_start(out=bias_bc[:], in_=bias.partition_broadcast(P))
         load_u(2, 0, 4)
         load_u(3, 0, 4)
 
@@ -117,50 +117,56 @@ def tile_sivalinear_kernel(tc, x, siva_u_t, siva_u_d, siva_s, siva_v_t, siva_v_d
 
         state = {}
 
-        def transposes(src, b):
+        def transposes(src, tiles):
             words = src[:].bitcast(F32)
             pt = psum.tile([P, 512], F32, name="pt", tag="w")
-            for sl in range(2):
+            for sl, a in enumerate(tiles):
                 for h in range(2):
-                    lo = 256 * sl + 128 * h
-                    nc.tensor.transpose(pt[:, lo : lo + 128], words[:, 512 * b + lo : 512 * b + lo + 128], ident[:])
+                    nc.tensor.transpose(
+                        pt[:, 256 * sl + 128 * h : 256 * sl + 128 * h + 128],
+                        words[:, 256 * a + 128 * h : 256 * a + 128 * h + 128],
+                        ident[:],
+                    )
             return pt
 
-        def t_u(c, b):
-            state["tu", c, b] = transposes(u_raw[c], b)
+        def t_u(c, tiles):
+            pt = transposes(u_raw[c], tiles)
+            for sl, a in enumerate(tiles):
+                state["tu", c, a] = (pt, sl)
 
-        def e_u(c, b):
-            if b == 0:
+        def e_u(c, a):
+            if a == 0:
                 state["ug", c] = grp.tile([P, 2048], BF16, name="ug", tag="ug", align_bytes=64)
-            ug = state["ug", c]
-            view = state["tu", c, b][:].bitcast(BF16).rearrange("p (s h o e) -> p s o h e", s=2, h=2, e=2)
-            for sl in range(2):
-                a = 2 * b + sl
-                nc.vector.tensor_tensor(
-                    out=ug[:, 512 * a : 512 * a + 512].rearrange("p (o h e) -> p o h e", h=2, e=2),
-                    in0=view[:, sl],
-                    in1=s4_b,
-                    op=ALU.mult,
-                )
+            pt, sl = state["tu", c, a]
+            view = pt[:].bitcast(BF16).rearrange("p (s h o e) -> p s o h e", s=2, h=2, e=2)
+            nc.vector.tensor_tensor(
+                out=state["ug", c][:, 512 * a : 512 * a + 512].rearrange("p (o h e) -> p o h e", h=2, e=2),
+                in0=view[:, sl],
+                in1=s4_b,
+                op=ALU.mult,
+            )
 
         def q_u(c, lo=0, hi=512):
             quantise(u_q[c], state["ug", c], lo, hi)
 
-        def r_v(g, h, eng):
-            if h == 0:
+        def r_v(g, h, eng, e=None):
+            if ("vg", g) not in state:
                 state["vg", g] = grp.tile([P, 2048], BF16, name="vg", tag="vg", align_bytes=64)
-            src = v_raw[g][:].rearrange("p (j h q e) -> p h e q j", j=4, h=2, e=2)
-            dst = state["vg", g][:].rearrange("p (h e q j) -> p h e q j", h=2, e=2, j=4)
+            src = v_raw[g][:].rearrange("p (j h q e) -> p h e q j", j=4, h=2, e=2)[:, h]
+            dst = state["vg", g][:].rearrange("p (h e q j) -> p h e q j", h=2, e=2, j=4)[:, h]
+            if e is not None:
+                src = src[:, e]
+                dst = dst[:, e]
             if eng == "v":
-                nc.vector.tensor_copy(out=dst[:, h], in_=src[:, h])
+                nc.vector.tensor_copy(out=dst, in_=src)
             else:
-                nc.scalar.copy(out=dst[:, h], in_=src[:, h])
+                nc.scalar.copy(out=dst, in_=src)
 
-        def q_v(g):
-            quantise(v_q[g], state["vg", g])
+        def q_v(g, lo=0, hi=512):
+            quantise(v_q[g], state["vg", g], lo, hi)
 
         def t_x(g, b):
-            state["tx", g, b] = transposes(x_raw[g], b)
+            state["tx", g, b] = transposes(x_raw[g], (2 * b, 2 * b + 1))
 
         def e_x(g, b, eng):
             if b == 0:
@@ -225,38 +231,33 @@ def tile_sivalinear_kernel(tc, x, siva_u_t, siva_u_d, siva_s, siva_v_t, siva_v_d
             )
             nc.sync.dma_start(out=of[128 * m : 128 * m + 128, 512 * c : 512 * c + 512], in_=res[:])
 
-        def b_mm(c):
-            pb = psum_o.tile([P, 512], F32, name="pb%d" % c, tag="o%d" % c)
-            nc.tensor.matmul(out=pb[:], lhsT=ones[:], rhs=bias_row[:, 512 * c : 512 * c + 512], start=True, stop=True)
-            state["pb", c] = pb
-
-        def b_ev(c):
-            nc.scalar.copy(out=bias_bc[:, 512 * c : 512 * c + 512], in_=state["pb", c][:])
-
-        for c in range(NC):
-            b_mm(c)
-        r_v(0, 0, "v")
-        r_v(0, 1, "s")
-        for c in range(NC):
-            b_ev(c)
-        t_u(0, 0)
-        q_v(0)
+        t_u(0, (0,))
         e_u(0, 0)
-        t_u(0, 1)
-        q_u(0, 0, 256)
+        r_v(0, 0, "v")
+        r_v(0, 1, "s", 1)
+        q_u(0, 0, 128)
+        r_v(0, 1, "v", 0)
+        q_v(0, 0, 256)
+        t_u(0, (1,))
         e_u(0, 1)
+        q_v(0, 256, 512)
+        q_u(0, 128, 256)
+        t_u(0, (2, 3))
+        e_u(0, 2)
+        e_u(0, 3)
         q_u(0, 256, 512)
         for s in range(STEPS):
             c, g = divmod(s, NG)
             last = s == STEPS - 1
+            if 1 <= s:
+                q_w(s - 1)
             if s + 1 < NG:
                 r_v(s + 1, 0, "v")
                 r_v(s + 1, 1, "v")
-                q_v(s + 1)
-            if 1 <= s:
-                q_w(s - 1)
             if 1 <= s <= NG:
                 q_x(s - 1)
+            if s + 1 < NG:
+                q_v(s + 1)
             if g == 3 and c + 1 < NC:
                 q_u(c + 1)
             for a in range(4):
@@ -270,8 +271,9 @@ def tile_sivalinear_kernel(tc, x, siva_u_t, siva_u_d, siva_s, siva_v_t, siva_v_d
                     e_x(s, b, "s")
             if g == 2 and c + 1 < NC:
                 for b in range(2):
-                    t_u(c + 1, b)
-                    e_u(c + 1, b)
+                    t_u(c + 1, (2 * b, 2 * b + 1))
+                    e_u(c + 1, 2 * b)
+                    e_u(c + 1, 2 * b + 1)
             closed = []
             for m in M_ORDER:
                 sm = s - LAGS[m]

@@ -51,7 +51,6 @@ def tile_sivalinear_kernel(tc, x, siva_u_t, siva_u_d, siva_s, siva_v_t, siva_v_d
         warm_in = const.tile([P, 1], F32, name="warm_in")
         warm_out = const.tile([P, 1], F32, name="warm_out")
         nc.vector.memset(warm_in[:], 0.0)
-        nc.scalar.copy(out=warm_out[:], in_=warm_in[:])
         ident = const.tile([P, P], F32, name="ident")
         make_identity(nc, ident[:])
 
@@ -59,13 +58,13 @@ def tile_sivalinear_kernel(tc, x, siva_u_t, siva_u_d, siva_s, siva_v_t, siva_v_d
         u_raw = [raw.tile([P, 4 * R], BF16, name="u_raw%d" % c) for c in range(NC)]
         x_raw = [raw.tile([P, NM * 512], BF16, name="x_raw%d" % g) for g in range(NG)]
 
-        def load_v(g):
+        def load_v(g, queue96):
             cols = slice(512 * g, 512 * g + 512)
             lo = v_raw[g][:, 0:1024].rearrange("q (e i) -> q e i", e=2)
             hi = v_raw[g][:, 1024:2048].rearrange("q (e i) -> q e i", e=2)
-            nc.sync.dma_start(out=lo[0:32], in_=siva_v_t[:, cols].rearrange("(q e) i -> q e i", e=2))
-            nc.sync.dma_start(out=lo[32:128], in_=siva_v_d[0:192, cols].rearrange("(q e) i -> q e i", e=2))
             nc.sync.dma_start(out=hi, in_=siva_v_d[192:448, cols].rearrange("(q e) i -> q e i", e=2))
+            nc.sync.dma_start(out=lo[0:32], in_=siva_v_t[:, cols].rearrange("(q e) i -> q e i", e=2))
+            queue96.dma_start(out=lo[32:128], in_=siva_v_d[0:192, cols].rearrange("(q e) i -> q e i", e=2))
 
         def load_u(c, a0, a1):
             rows = slice(512 * c + 128 * a0, 512 * c + 128 * a1)
@@ -81,14 +80,15 @@ def tile_sivalinear_kernel(tc, x, siva_u_t, siva_u_d, siva_s, siva_v_t, siva_v_d
             )
 
         load_u(0, 0, 1)
-        load_v(0)
+        load_v(0, nc.scalar)
+        nc.scalar.copy(out=warm_out[:], in_=warm_in[:])
         load_u(0, 1, 2)
         load_u(0, 2, 4)
-        load_v(1)
+        load_v(1, nc.sync)
         load_x(0)
-        load_v(2)
+        load_v(2, nc.sync)
         load_x(1)
-        load_v(3)
+        load_v(3, nc.sync)
         load_x(2)
         load_u(1, 0, 4)
         load_x(3)
@@ -234,9 +234,8 @@ def tile_sivalinear_kernel(tc, x, siva_u_t, siva_u_d, siva_s, siva_v_t, siva_v_d
         t_u(0, (0,))
         e_u(0, 0)
         r_v(0, 0, "v")
-        r_v(0, 1, "s", 1)
+        r_v(0, 1, "s")
         q_u(0, 0, 128)
-        r_v(0, 1, "v", 0)
         q_v(0, 0, 256)
         t_u(0, (1,))
         e_u(0, 1)

@@ -158,7 +158,9 @@ def tile_sivalinear_kernel(tc, x, siva_u_t, siva_u_d, siva_s, siva_v_t, siva_v_d
                 src = src[:, e]
                 dst = dst[:, e]
             if eng == "v":
-                nc.vector.tensor_copy(out=dst, in_=src)
+                nc.vector.tensor_copy(
+                    out=dst.rearrange("p e (c i) j -> p e c j i", i=4), in_=src.rearrange("p e (c i) j -> p e c j i", i=4)
+                )
             else:
                 nc.scalar.copy(out=dst, in_=src)
 

@@ -263,7 +263,7 @@ def tile_sivalinear_kernel(tc, x, siva_u_t, siva_u_d, siva_s, siva_v_t, siva_v_d
                 q_u(c + 1)
             for a in range(4):
                 m1(s, a)
-                e_w(s, a, "v" if ((a == 3 and s >= NG and s % V_EVERY == 1) or (last and a == 1)) else "s")
+                e_w(s, a, "v" if ((a == 3 and s % V_EVERY == 1) or (last and a == 1)) else "s")
                 if last and a % 2 == 1:
                     q_w(s, 128 * (a - 1), 128 * (a + 1))
             if s < NG:

from contextlib import ExitStack

import concourse.mybir as mybir
from concourse.masks import make_identity

F32 = mybir.dt.float32
BF16 = mybir.dt.bfloat16
U32 = mybir.dt.uint32
U8 = mybir.dt.uint8
FP8X4 = mybir.dt.float8_e4m3fn_x4
ALU = mybir.AluOpType

P = 128
TOK = 512
IN = 2048
OUT = 2048
R = 512
RT = 64
NG = 4
NC = 4
NM = 4
STEPS = NC * NG
LAGS = (1, 2, 2, 3)
M_ORDER = (3, 2, 1, 0)
V_EVERY = 2

FLOPS = 2 * OUT * IN * R + 2 * TOK * IN * OUT


def tile_sivalinear_kernel(tc, x, siva_u_t, siva_u_d, siva_s, siva_v_t, siva_v_d, bias, out):
    nc = tc.nc
    xf = x.flatten_outer_dims()
    of = out.flatten_outer_dims()

    with ExitStack() as ctx:
        const = ctx.enter_context(tc.tile_pool(name="const", bufs=1))
        raw = ctx.enter_context(tc.tile_pool(name="raw", bufs=1))
        grp = ctx.enter_context(tc.tile_pool(name="grp", bufs=2))
        wgp = ctx.enter_context(tc.tile_pool(name="wgp", bufs=4))
        keep = ctx.enter_context(tc.tile_pool(name="keep", bufs=1))
        resp = ctx.enter_context(tc.tile_pool(name="resp", bufs=4))
        psum = ctx.enter_context(tc.psum_pool(name="psum", bufs=4))
        psum_o = ctx.enter_context(tc.psum_pool(name="psum_o", bufs=1))
        ctx.enter_context(tc.manual_schedule())

        s4 = const.tile([P, 4], BF16, name="s4")
        nc.scalar.dma_start(
            out=s4[:].rearrange("p (h e) -> p h e", h=2),
            in_=siva_s.rearrange("(h p e) -> p h e", h=2, e=2),
        )
        warm_in = const.tile([P, 1], F32, name="warm_in")
        warm_out = const.tile([P, 1], F32, name="warm_out")
        nc.vector.memset(warm_in[:], 0.0)
        ident = const.tile([P, P], F32, name="ident")
        make_identity(nc, ident[:])

        v_raw = [raw.tile([P, 4 * 512], BF16, name="v_raw%d" % g) for g in range(NG)]
        u_raw = [raw.tile([P, 4 * R], BF16, name="u_raw%d" % c) for c in range(NC)]
        x_raw = [raw.tile([P, NM * 512], BF16, name="x_raw%d" % g) for g in range(NG)]

        def load_v(g, queue96):
            cols = slice(512 * g, 512 * g + 512)
            lo = v_raw[g][:, 0:1024].rearrange("q (e i) -> q e i", e=2)
            hi = v_raw[g][:, 1024:2048].rearrange("q (e i) -> q e i", e=2)
            nc.sync.dma_start(out=hi, in_=siva_v_d[192:448, cols].rearrange("(q e) i -> q e i", e=2))
            nc.sync.dma_start(out=lo[0:32], in_=siva_v_t[:, cols].rearrange("(q e) i -> q e i", e=2))
            queue96.dma_start(out=lo[32:128], in_=siva_v_d[0:192, cols].rearrange("(q e) i -> q e i", e=2))

        def load_u(c, a0, a1):
            rows = slice(512 * c + 128 * a0, 512 * c + 128 * a1)
            dst = u_raw[c][:].rearrange("p (a r) -> p a r", a=4)[:, a0:a1]
            nc.sync.dma_start(out=dst[:, :, 0:RT], in_=siva_u_t[rows, :].rearrange("(a p) r -> p a r", p=P))
            nc.sync.dma_start(out=dst[:, :, RT:R], in_=siva_u_d[rows, :].rearrange("(a p) r -> p a r", p=P))

        def load_x(g):
            cols = slice(512 * g, 512 * g + 512)
            nc.sync.dma_start(
                out=x_raw[g][:].rearrange("p (m i) -> p m i", m=NM),
                in_=xf[:, cols].rearrange("(m p) i -> p m i", p=P),
            )

        load_u(0, 0, 1)
        load_v(0, nc.scalar)
        nc.scalar.copy(out=warm_out[:], in_=warm_in[:])
        load_u(0, 1, 2)
        load_u(0, 2, 4)
        load_v(1, nc.sync)
        load_x(0)
        load_v(2, nc.sync)
        load_x(1)
        load_v(3, nc.sync)
        load_x(2)
        load_u(1, 0, 4)
        load_x(3)
        bias_bc = const.tile([P, OUT], BF16, name="bias_bc")
        nc.sync.dma_start(out=bias_bc[:], in_=bias.partition_broadcast(P))
        load_u(2, 0, 4)
        load_u(3, 0, 4)

        def codes(name):
            return (
                keep.tile([P, 512], U32, name=name + "_c", align_bytes=64),
                keep.tile([P, 512], U8, name=name + "_s", align_bytes=64),
            )

        u_q = [codes("u%d" % c) for c in range(NC)]
        v_q = [codes("v%d" % g) for g in range(NG)]
        x_q = [codes("x%d" % g) for g in range(NG)]
        w_q = [codes("w%d" % s) for s in range(STEPS)]

        def quantise(dst, src, lo=0, hi=512):
            nc.vector.quantize_mx(
                out=dst[0][:, lo:hi].bitcast(FP8X4), scales=dst[1][:, lo:hi], in_=src[:, 4 * lo : 4 * hi]
            )

        s4_b = s4[:].rearrange("p (o h e) -> p o h e", o=1, h=2).to_broadcast([P, P, 2, 2])

        state = {}

        def transposes(src, tiles):
            words = src[:].bitcast(F32)
            pt = psum.tile([P, 512], F32, name="pt", tag="w")
            for sl, a in enumerate(tiles):
                for h in range(2):
                    nc.tensor.transpose(
                        pt[:, 256 * sl + 128 * h : 256 * sl + 128 * h + 128],
                        words[:, 256 * a + 128 * h : 256 * a + 128 * h + 128],
                        ident[:],
                    )
            return pt

        def t_u(c, tiles):
            pt = transposes(u_raw[c], tiles)
            for sl, a in enumerate(tiles):
                state["tu", c, a] = (pt, sl)

        def e_u(c, a):
            if a == 0:
                state["ug", c] = grp.tile([P, 2048], BF16, name="ug", tag="ug", align_bytes=64)
            pt, sl = state["tu", c, a]
            view = pt[:].bitcast(BF16).rearrange("p (s h o e) -> p s o h e", s=2, h=2, e=2)
            nc.vector.tensor_tensor(
                out=state["ug", c][:, 512 * a : 512 * a + 512].rearrange("p (o h e) -> p o h e", h=2, e=2),
                in0=view[:, sl],
                in1=s4_b,
                op=ALU.mult,
            )

        def q_u(c, lo=0, hi=512):
            quantise(u_q[c], state["ug", c], lo, hi)

        def r_v(g, h, eng, e=None):
            if ("vg", g) not in state:
                state["vg", g] = grp.tile([P, 2048], BF16, name="vg", tag="vg", align_bytes=64)
            src = v_raw[g][:].rearrange("p (j h q e) -> p h e q j", j=4, h=2, e=2)[:, h]
            dst = state["vg", g][:].rearrange("p (h e q j) -> p h e q j", h=2, e=2, j=4)[:, h]
            if e is not None:
                src = src[:, e]
                dst = dst[:, e]
            if eng == "v":
                nc.vector.tensor_copy(
                    out=dst.rearrange("p e (c i) j -> p e c j i", i=4), in_=src.rearrange("p e (c i) j -> p e c j i", i=4)
                )
            else:
                nc.scalar.copy(out=dst, in_=src)

        def q_v(g, lo=0, hi=512):
            quantise(v_q[g], state["vg", g], lo, hi)

        def t_x(g, b):
            state["tx", g, b] = transposes(x_raw[g], (2 * b, 2 * b + 1))

        def e_x(g, b, eng):
            if b == 0:
                state["xg", g] = grp.tile([P, 2048], BF16, name="xg", tag="xg", align_bytes=64)
            xw = state["xg", g][:].bitcast(F32)
            dst = xw[:, 512 * b : 512 * b + 512].rearrange("p (s k h) -> p s k h", s=2, h=2)
            src = state["tx", g, b][:].rearrange("p (s h k) -> p s k h", s=2, h=2)
            if eng == "v":
                nc.vector.tensor_copy(out=dst, in_=src)
            else:
                nc.scalar.copy(out=dst, in_=src)

        def q_x(g):
            quantise(x_q[g], state["xg", g])

        def m1(s, a):
            c, g = divmod(s, NG)
            pw = psum.tile([P, 512], F32, name="pw", tag="w")
            for t in range(4):
                nc.tensor.matmul_mx(
                    out=pw[:, 128 * t : 128 * t + 128],
                    lhsT=v_q[g][0][:, 128 * t : 128 * t + 128].bitcast(FP8X4),
                    lhsT_scale=v_q[g][1][:, 128 * t : 128 * t + 128],
                    rhs=u_q[c][0][:, 128 * a : 128 * a + 128].bitcast(FP8X4),
                    rhs_scale=u_q[c][1][:, 128 * a : 128 * a + 128],
                    start=True,
                    stop=True,
                )
            state["pw", s, a] = pw

        def e_w(s, a, eng):
            if a == 0:
                state["wg", s] = wgp.tile([P, 2048], BF16, name="wg", tag="wg", align_bytes=64)
            dst = state["wg", s][:, 512 * a : 512 * a + 512].rearrange("p (o t) -> p o t", t=4)
            src = state["pw", s, a][:].rearrange("p (t o) -> p o t", t=4)
            if eng == "v":
                nc.vector.tensor_copy(out=dst, in_=src)
            else:
                nc.scalar.copy(out=dst, in_=src)

        def q_w(s, lo=0, hi=512):
            quantise(w_q[s], state["wg", s], lo, hi)

        def m2(s, m):
            c, g = divmod(s, NG)
            if g == 0:
                state["po", m] = psum_o.tile([P, 512], F32, name="po%d" % m, tag="o%d" % m)
            nc.tensor.matmul_mx(
                out=state["po", m][:],
                lhsT=x_q[g][0][:, 128 * m : 128 * m + 128].bitcast(FP8X4),
                lhsT_scale=x_q[g][1][:, 128 * m : 128 * m + 128],
                rhs=w_q[s][0][:].bitcast(FP8X4),
                rhs_scale=w_q[s][1][:],
                start=(g == 0),
                stop=(g == NG - 1),
            )

        def e_o(c, m):
            res = resp.tile([P, 512], F32, name="res", tag="res")
            nc.vector.tensor_tensor(
                out=res[:], in0=state["po", m][:], in1=bias_bc[:, 512 * c : 512 * c + 512], op=ALU.add
            )
            nc.sync.dma_start(out=of[128 * m : 128 * m + 128, 512 * c : 512 * c + 512], in_=res[:])

        t_u(0, (0,))
        e_u(0, 0)
        r_v(0, 0, "v")
        r_v(0, 1, "s")
        q_u(0, 0, 128)
        q_v(0, 0, 256)
        t_u(0, (1,))
        e_u(0, 1)
        q_v(0, 256, 512)
        q_u(0, 128, 256)
        t_u(0, (2, 3))
        e_u(0, 2)
        e_u(0, 3)
        q_u(0, 256, 512)
        for s in range(STEPS):
            c, g = divmod(s, NG)
            last = s == STEPS - 1
            if 1 <= s:
                q_w(s - 1)
            if s + 1 < NG:
                r_v(s + 1, 0, "v")
                r_v(s + 1, 1, "v")
            if 1 <= s <= NG:
                q_x(s - 1)
            if s + 1 < NG:
                q_v(s + 1)
            if g == 3 and c + 1 < NC:
                q_u(c + 1)
            for a in range(4):
                m1(s, a)
                e_w(s, a, "v" if ((a == 3 and s % V_EVERY == 1) or (last and a == 1)) else "s")
                if last and a % 2 == 1:
                    q_w(s, 128 * (a - 1), 128 * (a + 1))
            if s < NG:
                for b in range(2):
                    t_x(s, b)
                    e_x(s, b, "s")
            if g == 2 and c + 1 < NC:
                for b in range(2):
                    t_u(c + 1, (2 * b, 2 * b + 1))
                    e_u(c + 1, 2 * b)
                    e_u(c + 1, 2 * b + 1)
            closed = []
            for m in M_ORDER:
                sm = s - LAGS[m]
                if 0 <= sm:
                    m2(sm, m)
                    if sm % NG == NG - 1:
                        closed.append((sm // NG, m))
            for cm in closed:
                e_o(cm[0], cm[1])
        for m in M_ORDER:
            for sm in range(STEPS - LAGS[m], STEPS - 1):
                m2(sm, m)
        for m in M_ORDER:
            m2(STEPS - 1, m)
            e_o(NC - 1, m)
